import numpy as np
import ml_dtypes


def mxq(x, axis, fmt="e4m3"):
    dtype, down = {"e4m3": (ml_dtypes.float8_e4m3fn, 7), "e5m2": (ml_dtypes.float8_e5m2, 14)}[fmt]
    v = np.moveaxis(np.asarray(x, np.float32).astype(ml_dtypes.bfloat16).astype(np.float64), axis, -1)
    blocks = v.reshape(v.shape[:-1] + (-1, 32))
    amax = np.abs(blocks).max(-1, keepdims=True)
    byte = np.maximum(np.where(amax > 0, np.frexp(amax)[1] - 1 + 127, 0) - down, 1)
    scale = np.exp2(byte - 127.0)
    codes = (blocks / scale).astype(np.float32).astype(dtype).astype(np.float64)
    return np.moveaxis((codes * scale).reshape(v.shape), -1, axis)


WIDE = False


def mx_kscale(k):
    if not WIDE:
        return np.ones(k)
    levels = np.array([10, -10, 5, -5, 0])
    if k % 512:
        return np.exp2(np.random.permutation(np.resize(levels, k // 32))).repeat(32)
    a = np.empty((k // 512, 16))
    for p in range(k // 512):
        a[p, :8] = np.random.permutation(np.resize(levels, 8))
        for g in range(8):
            far = levels[np.abs(levels - a[p, g]) >= 10]
            a[p, g + 8] = far[np.random.randint(len(far))]
    return np.exp2(a.ravel()).repeat(32)


BF16 = ml_dtypes.bfloat16


def bf(x):
    return np.asarray(x, np.float32).astype(BF16)


def f64(x):
    return np.asarray(x).astype(np.float64)


S, B, D, H, F = 1024, 4, 512, 2, 2048
HD = D // H
EPS = 1e-8


def rmsnorm(x, w):
    ms = np.mean(x * x, axis=-1, keepdims=True)
    return w * (x / np.sqrt(ms + EPS))


def heads(t):
    return t.reshape(S, B, H, HD).transpose(1, 2, 0, 3)


def setup_inputs():
    s = mx_kscale(D)
    return {"x": bf(np.random.standard_normal((S, B, D))),
            "w_norm1": bf((1.0 + 0.1 * np.random.standard_normal(D)) * s),
            "in_proj_w": bf(np.random.standard_normal((3 * D, D)) / np.sqrt(D) / s[None, :]),
            "in_proj_b": bf(np.random.standard_normal(3 * D) * 0.3)}


def reference(x, w_norm1, in_proj_w, in_proj_b):
    h = rmsnorm(f64(x), f64(w_norm1))
    qkv = (mxq(h, 2, "e4m3") @ mxq(f64(in_proj_w), 1, "e4m3").T) + f64(in_proj_b)
    q, k, v = np.split(qkv, 3, axis=-1)
    return heads(q), heads(k), heads(v)

@@ -1,0 +1,182 @@
+from contextlib import ExitStack
+
+import concourse.mybir as mybir
+from concourse.masks import make_identity
+
+F32 = mybir.dt.float32
+BF16 = mybir.dt.bfloat16
+U32 = mybir.dt.uint32
+U8 = mybir.dt.uint8
+FP8X4 = mybir.dt.float8_e4m3fn_x4
+ACT = mybir.ActivationFunctionType
+ALU = mybir.AluOpType
+
+P = 128
+S, B, D = 1024, 4, 512
+HEADS, HD = 2, 256
+EPS = 1e-8
+PACK = 4
+ROWS = S // P
+CHUNK = 4
+PAIR = 2
+N_CHUNKS = B * ROWS // CHUNK
+W_TILES = D // P
+
+FLOPS = 2 * S * B * D * 3 * D
+
+
+def tile_transformerblock_pa_t_kernel(tc, x, w_norm1, in_proj_w, in_proj_b, out_0, out_1, out_2):
+    nc = tc.nc
+    outs = [out_0, out_1, out_2]
+    x_view = x.rearrange("(p j) b d -> p j b d", j=ROWS)
+    w_view = in_proj_w.rearrange("(c a p) d -> c p a d", c=3, a=W_TILES)
+
+    with ExitStack() as stack:
+        const = stack.enter_context(tc.tile_pool(name="const", bufs=1))
+        xin = stack.enter_context(tc.tile_pool(name="xin", bufs=N_CHUNKS))
+        wprep = stack.enter_context(tc.tile_pool(name="wprep", bufs=3))
+        stat = stack.enter_context(tc.tile_pool(name="stat", bufs=4))
+        work = stack.enter_context(tc.tile_pool(name="work", bufs=6))
+        result = stack.enter_context(tc.tile_pool(name="result", bufs=6))
+        psum_t = stack.enter_context(tc.psum_pool(name="psum_t", bufs=2))
+        psum_o = stack.enter_context(tc.psum_pool(name="psum_o", bufs=6))
+
+        gain_row = const.tile([P, D], BF16)
+        nc.vector.memset(gain_row[:], 0.0)
+        nc.sync.dma_start(out=gain_row[0:1, :], in_=w_norm1.unsqueeze(0))
+        bias_row = const.tile([P, 3 * D], BF16)
+        nc.vector.memset(bias_row[:], 0.0)
+
+        def load_x(n):
+            b, jq = divmod(n, ROWS // CHUNK)
+            xc = xin.tile([P, CHUNK, D], BF16, name="xc")
+            nc.sync.dma_start(out=xc[:], in_=x_view[:, jq * CHUNK : (jq + 1) * CHUNK, b, :])
+            return xc
+
+        x_chunks = [load_x(0)]
+        nc.sync.dma_start(out=bias_row[0:1, :], in_=in_proj_b.unsqueeze(0))
+        w_raws = []
+        for c in range(3):
+            w_raw = wprep.tile([P, W_TILES, D], BF16, name="w_raw")
+            nc.sync.dma_start(out=w_raw[:], in_=w_view[c])
+            w_raws.append(w_raw)
+        for n in range(1, N_CHUNKS):
+            x_chunks.append(load_x(n))
+
+        ident_f32 = const.tile([P, P], F32)
+        make_identity(nc, ident_f32[:])
+        eps = const.tile([P, 1], F32)
+        nc.vector.memset(eps[:], EPS)
+        warm = const.tile([P, 1], F32)
+        nc.scalar.activation(out=warm[:], in_=eps[:], func=ACT.Sqrt)
+
+        ones = const.tile([P, P], BF16)
+        nc.vector.memset(ones[:], 1.0)
+
+        def spread(row, everywhere):
+            copies = psum_o.tile([P, D], F32, name="copies", tag="acc")
+            nc.tensor.matmul(out=copies[:], lhsT=ones[:], rhs=row, start=True, stop=True)
+            nc.vector.tensor_copy(out=everywhere, in_=copies[:])
+
+        gain = const.tile([P, D], BF16)
+        spread(gain_row[:], gain[:])
+        bias = const.tile([P, 3 * D], BF16)
+        for c in range(3):
+            spread(bias_row[:, c * D : (c + 1) * D], bias[:, c * D : (c + 1) * D])
+
+        w_codes, w_scales = [], []
+
+        def prepare_w(c):
+            w_grouped = wprep.tile([P, D * PACK], BF16, name="w_grouped", align_bytes=64)
+            words = w_grouped[:].bitcast(F32).rearrange("p (a r u) -> p a r u", a=W_TILES, u=2)
+            for half in range(W_TILES // PAIR):
+                wt = psum_t.tile([P, PAIR, 2, P], F32, name="wt", tag="t")
+                for i in range(PAIR):
+                    row_words = w_raws[c][:, half * PAIR + i, :].bitcast(F32)
+                    for u in range(2):
+                        nc.tensor.transpose(wt[:, i, u, :], row_words[:, u : 2 * P : 2], ident_f32[:])
+                nc.vector.tensor_copy(
+                    out=words[:, half * PAIR : (half + 1) * PAIR, :, :],
+                    in_=wt[:].rearrange("p a u r -> p a r u"),
+                )
+            codes = const.tile([P, D], U32, name="w_codes%d" % c, align_bytes=64)
+            scales = const.tile([P, D], U8, name="w_scales%d" % c, align_bytes=64)
+            nc.vector.quantize_mx(out=codes[:].bitcast(FP8X4), scales=scales[:], in_=w_grouped[:])
+            w_codes.append(codes)
+            w_scales.append(scales)
+
+        def front(n):
+            xc = x_chunks[n]
+            sumsq = stat.tile([P, CHUNK], F32, name="sumsq")
+            gained = []
+            for j in range(CHUNK):
+                y = work.tile([P, D], F32, name="y")
+                nc.gpsimd.tensor_tensor(out=y[:], in0=xc[:, j, :], in1=gain[:], op=ALU.mult)
+                gained.append(y)
+                squares = stat.tile([P, D], BF16, name="squares")
+                nc.scalar.activation(out=squares[:], in_=xc[:, j, :], func=ACT.Square, accum_out=sumsq[:, j : j + 1])
+            rms = stat.tile([P, CHUNK], F32, name="rms")
+            nc.scalar.activation(out=rms[:], in_=sumsq[:], func=ACT.Sqrt, scale=1.0 / D, bias=eps[:])
+            rstd = stat.tile([P, CHUNK], F32, name="rstd")
+            nc.vector.reciprocal(out=rstd[:], in_=rms[:])
+
+            operands = []
+            for pair in range(CHUNK // PAIR):
+                ht = psum_t.tile([P, PAIR, 2, P], F32, name="ht", tag="t")
+                for i in range(PAIR):
+                    j = pair * PAIR + i
+                    h = work.tile([P, D], BF16, name="h")
+                    nc.scalar.activation(out=h[:], in_=gained[j][:], func=ACT.Copy, scale=rstd[:, j : j + 1])
+                    h_words = h[:].bitcast(F32)
+                    for u in range(2):
+                        nc.tensor.transpose(ht[:, i, u, :], h_words[:, u : 2 * P : 2], ident_f32[:])
+                grouped = work.tile([P, PAIR * P * PACK], BF16, name="grouped", align_bytes=64)
+                nc.scalar.copy(
+                    out=grouped[:].bitcast(F32).rearrange("p (i r u) -> p i r u", i=PAIR, u=2),
+                    in_=ht[:].rearrange("p i u r -> p i r u"),
+                )
+                codes = work.tile([P, PAIR * P], U32, name="h_codes", align_bytes=64)
+                scales = work.tile([P, PAIR * P], U8, name="h_scales", align_bytes=64)
+                nc.vector.quantize_mx(
+                    out=codes[:].bitcast(FP8X4),
+                    scales=scales[:],
+                    in_=grouped[:],
+                )
+                operands.append((codes, scales))
+            return operands
+
+        def back(n, operands):
+            b, jq = divmod(n, ROWS // CHUNK)
+            for c in range(3):
+                res = result.tile([P, HEADS, CHUNK, HD], F32, name="res")
+                bias_c = bias[:, c * D : (c + 1) * D].rearrange("p (h d) -> p h d", h=HEADS)
+                for j in range(CHUNK):
+                    codes, scales = operands[j // PAIR]
+                    cols = slice((j % PAIR) * P, (j % PAIR + 1) * P)
+                    acc = psum_o.tile([P, D], F32, name="acc", tag="acc")
+                    nc.tensor.matmul_mx(
+                        out=acc[:],
+                        lhsT=codes[:, cols].bitcast(FP8X4),
+                        lhsT_scale=scales[:, cols],
+                        rhs=w_codes[c][:].bitcast(FP8X4),
+                        rhs_scale=w_scales[c][:],
+                        start=True,
+                        stop=True,
+                    )
+                    nc.vector.tensor_tensor(
+                        out=res[:, :, j, :],
+                        in0=acc[:].rearrange("p (h d) -> p h d", h=HEADS),
+                        in1=bias_c,
+                        op=ALU.add,
+                    )
+                out_view = outs[c][b].rearrange("h (p j) d -> p h j d", j=ROWS)
+                nc.sync.dma_start(out=out_view[:, :, jq * CHUNK : (jq + 1) * CHUNK, :], in_=res[:])
+
+        prepare_w(0)
+        ready = front(0)
+        prepare_w(1)
+        prepare_w(2)
+        for n in range(N_CHUNKS):
+            following = front(n + 1) if n + 1 < N_CHUNKS else None
+            back(n, ready)
+            ready = following

@@ -7,6 +7,7 @@ F32 = mybir.dt.float32
 BF16 = mybir.dt.bfloat16
 U32 = mybir.dt.uint32
 U8 = mybir.dt.uint8
+I32 = mybir.dt.int32
 FP8X4 = mybir.dt.float8_e4m3fn_x4
 ACT = mybir.ActivationFunctionType
 ALU = mybir.AluOpType
@@ -20,6 +21,11 @@ ROWS = S // P
 CHUNK = 4
 PAIR = 2
 N_CHUNKS = B * ROWS // CHUNK
+N_PAIRS = B * ROWS // PAIR
+CHUNK_BANKS = 3 * CHUNK
+SHARED = 5
+GROUP = 3
+N_GROUPS = N_CHUNKS * CHUNK_BANKS // GROUP
 W_TILES = D // P
 
 FLOPS = 2 * S * B * D * 3 * D
@@ -35,7 +41,7 @@ def tile_transformerblock_pa_t_kernel(tc, x, w_norm1, in_proj_w, in_proj_b, out_
         const = stack.enter_context(tc.tile_pool(name="const", bufs=1))
         xin = stack.enter_context(tc.tile_pool(name="xin", bufs=N_CHUNKS))
         wprep = stack.enter_context(tc.tile_pool(name="wprep", bufs=3))
-        stat = stack.enter_context(tc.tile_pool(name="stat", bufs=4))
+        stat = stack.enter_context(tc.tile_pool(name="stat", bufs=6))
         work = stack.enter_context(tc.tile_pool(name="work", bufs=6))
         result = stack.enter_context(tc.tile_pool(name="result", bufs=6))
         psum_t = stack.enter_context(tc.psum_pool(name="psum_t", bufs=2))
@@ -45,7 +51,7 @@ def tile_transformerblock_pa_t_kernel(tc, x, w_norm1, in_proj_w, in_proj_b, out_
         nc.vector.memset(gain_row[:], 0.0)
         nc.sync.dma_start(out=gain_row[0:1, :], in_=w_norm1.unsqueeze(0))
         bias_row = const.tile([P, 3 * D], BF16)
-        nc.vector.memset(bias_row[:], 0.0)
+        nc.gpsimd.memset(bias_row[:].bitcast(I32), 0)
 
         def load_x(n):
             b, jq = divmod(n, ROWS // CHUNK)
@@ -53,14 +59,18 @@ def tile_transformerblock_pa_t_kernel(tc, x, w_norm1, in_proj_w, in_proj_b, out_
             nc.sync.dma_start(out=xc[:], in_=x_view[:, jq * CHUNK : (jq + 1) * CHUNK, b, :])
             return xc
 
-        x_chunks = [load_x(0)]
-        nc.sync.dma_start(out=bias_row[0:1, :], in_=in_proj_b.unsqueeze(0))
-        w_raws = []
-        for c in range(3):
+        def load_w(c):
             w_raw = wprep.tile([P, W_TILES, D], BF16, name="w_raw")
             nc.sync.dma_start(out=w_raw[:], in_=w_view[c])
-            w_raws.append(w_raw)
-        for n in range(1, N_CHUNKS):
+            return w_raw
+
+        x_chunks = [load_x(0)]
+        w_raws = [load_w(0)]
+        x_chunks.append(load_x(1))
+        nc.sync.dma_start(out=bias_row[0:1, :], in_=in_proj_b.unsqueeze(0))
+        w_raws.append(load_w(1))
+        w_raws.append(load_w(2))
+        for n in range(2, N_CHUNKS):
             x_chunks.append(load_x(n))
 
         ident_f32 = const.tile([P, P], F32)
@@ -72,111 +82,211 @@ def tile_transformerblock_pa_t_kernel(tc, x, w_norm1, in_proj_w, in_proj_b, out_
 
         ones = const.tile([P, P], BF16)
         nc.vector.memset(ones[:], 1.0)
+        gain = const.tile([P, D], BF16)
+        bias = const.tile([P, 3 * D], BF16)
 
-        def spread(row, everywhere):
+        def spread(row):
             copies = psum_o.tile([P, D], F32, name="copies", tag="acc")
             nc.tensor.matmul(out=copies[:], lhsT=ones[:], rhs=row, start=True, stop=True)
-            nc.vector.tensor_copy(out=everywhere, in_=copies[:])
+            return copies
 
-        gain = const.tile([P, D], BF16)
-        spread(gain_row[:], gain[:])
-        bias = const.tile([P, 3 * D], BF16)
-        for c in range(3):
-            spread(bias_row[:, c * D : (c + 1) * D], bias[:, c * D : (c + 1) * D])
+        def spread_bias(c):
+            cols = slice(c * D, (c + 1) * D)
+            copies = spread(bias_row[:, cols])
+            nc.scalar.copy(out=bias[:, cols], in_=copies[:])
 
-        w_codes, w_scales = [], []
+        w_codes, w_scales, w_banks = {}, {}, {}
 
-        def prepare_w(c):
-            w_grouped = wprep.tile([P, D * PACK], BF16, name="w_grouped", align_bytes=64)
-            words = w_grouped[:].bitcast(F32).rearrange("p (a r u) -> p a r u", a=W_TILES, u=2)
+        def transpose_w(c):
+            w_banks[c] = []
             for half in range(W_TILES // PAIR):
-                wt = psum_t.tile([P, PAIR, 2, P], F32, name="wt", tag="t")
+                wt = psum_o.tile([P, PAIR, 2, P], F32, name="wt", tag="acc")
                 for i in range(PAIR):
                     row_words = w_raws[c][:, half * PAIR + i, :].bitcast(F32)
                     for u in range(2):
                         nc.tensor.transpose(wt[:, i, u, :], row_words[:, u : 2 * P : 2], ident_f32[:])
-                nc.vector.tensor_copy(
+                w_banks[c].append(wt)
+
+        def quantise_w(c, copies):
+            w_grouped = wprep.tile([P, D * PACK], BF16, name="w_grouped", align_bytes=64)
+            words = w_grouped[:].bitcast(F32).rearrange("p (a r u) -> p a r u", a=W_TILES, u=2)
+            for half, copy in enumerate(copies):
+                copy(
                     out=words[:, half * PAIR : (half + 1) * PAIR, :, :],
-                    in_=wt[:].rearrange("p a u r -> p a r u"),
+                    in_=w_banks[c][half][:].rearrange("p a u r -> p a r u"),
                 )
             codes = const.tile([P, D], U32, name="w_codes%d" % c, align_bytes=64)
             scales = const.tile([P, D], U8, name="w_scales%d" % c, align_bytes=64)
             nc.vector.quantize_mx(out=codes[:].bitcast(FP8X4), scales=scales[:], in_=w_grouped[:])
-            w_codes.append(codes)
-            w_scales.append(scales)
+            w_codes[c] = codes
+            w_scales[c] = scales
 
-        def front(n):
-            xc = x_chunks[n]
-            sumsq = stat.tile([P, CHUNK], F32, name="sumsq")
-            gained = []
-            for j in range(CHUNK):
-                y = work.tile([P, D], F32, name="y")
-                nc.gpsimd.tensor_tensor(out=y[:], in0=xc[:, j, :], in1=gain[:], op=ALU.mult)
-                gained.append(y)
+        sums, roots, rstds, products, hs, banks, groupeds, operands = {}, {}, {}, {}, {}, {}, {}, {}
+
+        def x_tile(q, i):
+            return x_chunks[q * PAIR // CHUNK][:, q * PAIR % CHUNK + i, :]
+
+        def square_sums(q):
+            sums[q] = stat.tile([P, PAIR], F32, name="sumsq")
+            for i in range(PAIR):
                 squares = stat.tile([P, D], BF16, name="squares")
-                nc.scalar.activation(out=squares[:], in_=xc[:, j, :], func=ACT.Square, accum_out=sumsq[:, j : j + 1])
-            rms = stat.tile([P, CHUNK], F32, name="rms")
-            nc.scalar.activation(out=rms[:], in_=sumsq[:], func=ACT.Sqrt, scale=1.0 / D, bias=eps[:])
-            rstd = stat.tile([P, CHUNK], F32, name="rstd")
-            nc.vector.reciprocal(out=rstd[:], in_=rms[:])
+                nc.scalar.activation(out=squares[:], in_=x_tile(q, i), func=ACT.Square, accum_out=sums[q][:, i : i + 1])
 
-            operands = []
-            for pair in range(CHUNK // PAIR):
-                ht = psum_t.tile([P, PAIR, 2, P], F32, name="ht", tag="t")
-                for i in range(PAIR):
-                    j = pair * PAIR + i
-                    h = work.tile([P, D], BF16, name="h")
-                    nc.scalar.activation(out=h[:], in_=gained[j][:], func=ACT.Copy, scale=rstd[:, j : j + 1])
-                    h_words = h[:].bitcast(F32)
-                    for u in range(2):
-                        nc.tensor.transpose(ht[:, i, u, :], h_words[:, u : 2 * P : 2], ident_f32[:])
-                grouped = work.tile([P, PAIR * P * PACK], BF16, name="grouped", align_bytes=64)
-                nc.scalar.copy(
-                    out=grouped[:].bitcast(F32).rearrange("p (i r u) -> p i r u", i=PAIR, u=2),
-                    in_=ht[:].rearrange("p i u r -> p i r u"),
+        def root(q):
+            roots[q] = stat.tile([P, PAIR], F32, name="rms")
+            nc.scalar.activation(out=roots[q][:], in_=sums[q][:], func=ACT.Sqrt, scale=1.0 / D, bias=eps[:])
+
+        def invert(q):
+            rstds[q] = stat.tile([P, PAIR], F32, name="rstd")
+            nc.vector.reciprocal(out=rstds[q][:], in_=roots[q][:])
+
+        def multiply_gain(q):
+            products[q] = []
+            for i in range(PAIR):
+                y = work.tile([P, D], F32, name="y")
+                nc.gpsimd.tensor_tensor(out=y[:], in0=x_tile(q, i), in1=gain[:], op=ALU.mult)
+                products[q].append(y)
+
+        def scale(q):
+            hs[q] = []
+            for i in range(PAIR):
+                h = work.tile([P, D], BF16, name="h")
+                nc.scalar.activation(out=h[:], in_=products[q][i][:], func=ACT.Copy, scale=rstds[q][:, i : i + 1])
+                hs[q].append(h)
+
+        def scale_and_gain(q):
+            hs[q] = []
+            for i in range(PAIR):
+                h = work.tile([P, D], BF16, name="h")
+                nc.vector.scalar_tensor_tensor(
+                    out=h[:], in0=x_tile(q, i), scalar=rstds[q][:, i : i + 1], in1=gain[:], op0=ALU.mult, op1=ALU.mult
                 )
-                codes = work.tile([P, PAIR * P], U32, name="h_codes", align_bytes=64)
-                scales = work.tile([P, PAIR * P], U8, name="h_scales", align_bytes=64)
-                nc.vector.quantize_mx(
-                    out=codes[:].bitcast(FP8X4),
-                    scales=scales[:],
-                    in_=grouped[:],
+                hs[q].append(h)
+
+        def transpose(q):
+            ht = psum_t.tile([P, PAIR, 2, P], F32, name="ht")
+            for i in range(PAIR):
+                h_words = hs[q][i][:].bitcast(F32)
+                for u in range(2):
+                    nc.tensor.transpose(ht[:, i, u, :], h_words[:, u : 2 * P : 2], ident_f32[:])
+            banks[q] = ht
+
+        def empty(q):
+            grouped = work.tile([P, PAIR * P * PACK], BF16, name="grouped", align_bytes=64)
+            nc.scalar.copy(
+                out=grouped[:].bitcast(F32).rearrange("p (i r u) -> p i r u", i=PAIR, u=2),
+                in_=banks[q][:].rearrange("p i u r -> p i r u"),
+            )
+            groupeds[q] = grouped
+
+        def quantise(q):
+            codes = work.tile([P, PAIR * P], U32, name="h_codes", align_bytes=64)
+            scales = work.tile([P, PAIR * P], U8, name="h_scales", align_bytes=64)
+            nc.vector.quantize_mx(out=codes[:].bitcast(FP8X4), scales=scales[:], in_=groupeds[q][:])
+            operands[q] = (codes, scales)
+
+        accs, results = {}, {}
+
+        def place(k):
+            n, r = divmod(k, CHUNK_BANKS)
+            c, j = divmod(r, CHUNK)
+            return n, c, j
+
+        def multiply(g):
+            for k in range(g * GROUP, (g + 1) * GROUP):
+                n, c, j = place(k)
+                codes, scales = operands[(n * CHUNK + j) // PAIR]
+                cols = slice((j % PAIR) * P, (j % PAIR + 1) * P)
+                acc = psum_o.tile([P, D], F32, name="acc", tag="acc")
+                nc.tensor.matmul_mx(
+                    out=acc[:],
+                    lhsT=codes[:, cols].bitcast(FP8X4),
+                    lhsT_scale=scales[:, cols],
+                    rhs=w_codes[c][:].bitcast(FP8X4),
+                    rhs_scale=w_scales[c][:],
+                    start=True,
+                    stop=True,
                 )
-                operands.append((codes, scales))
-            return operands
+                accs[k] = acc
 
-        def back(n, operands):
-            b, jq = divmod(n, ROWS // CHUNK)
-            for c in range(3):
-                res = result.tile([P, HEADS, CHUNK, HD], F32, name="res")
-                bias_c = bias[:, c * D : (c + 1) * D].rearrange("p (h d) -> p h d", h=HEADS)
-                for j in range(CHUNK):
-                    codes, scales = operands[j // PAIR]
-                    cols = slice((j % PAIR) * P, (j % PAIR + 1) * P)
-                    acc = psum_o.tile([P, D], F32, name="acc", tag="acc")
-                    nc.tensor.matmul_mx(
-                        out=acc[:],
-                        lhsT=codes[:, cols].bitcast(FP8X4),
-                        lhsT_scale=scales[:, cols],
-                        rhs=w_codes[c][:].bitcast(FP8X4),
-                        rhs_scale=w_scales[c][:],
-                        start=True,
-                        stop=True,
-                    )
-                    nc.vector.tensor_tensor(
-                        out=res[:, :, j, :],
-                        in0=acc[:].rearrange("p (h d) -> p h d", h=HEADS),
-                        in1=bias_c,
-                        op=ALU.add,
-                    )
-                out_view = outs[c][b].rearrange("h (p j) d -> p h j d", j=ROWS)
-                nc.sync.dma_start(out=out_view[:, :, jq * CHUNK : (jq + 1) * CHUNK, :], in_=res[:])
+        def add_bias(g):
+            for k in [g * GROUP + i for i in (2, 0, 1)]:
+                n, c, j = place(k)
+                if (n, c) not in results:
+                    results[n, c] = (result.tile([P, HEADS, CHUNK, HD], F32, name="res"), [])
+                res, done = results[n, c]
+                sums_in = accs[k][:].rearrange("p (h d) -> p h d", h=HEADS)
+                bias_in = bias[:, c * D : (c + 1) * D].rearrange("p (h d) -> p h d", h=HEADS)
+                if k % CHUNK_BANKS == SHARED:
+                    nc.scalar.copy(out=res[:, :, j, :], in_=sums_in)
+                    nc.gpsimd.tensor_tensor(out=res[:, :, j, :], in0=res[:, :, j, :], in1=bias_in, op=ALU.add)
+                else:
+                    nc.vector.tensor_tensor(out=res[:, :, j, :], in0=sums_in, in1=bias_in, op=ALU.add)
+                done.append(j)
+                last = n == N_CHUNKS - 1 and c == 2
+                for part in [(0, 1), (2, 3)] if last else [(0, 1, 2, 3)]:
+                    if j in part and all(i in done for i in part):
+                        b, jq = divmod(n, ROWS // CHUNK)
+                        first, end = part[0], part[-1] + 1
+                        out_view = outs[c][b].rearrange("h (p j) d -> p h j d", j=ROWS)
+                        out_part = out_view[:, :, jq * CHUNK + first : jq * CHUNK + end, :]
+                        nc.sync.dma_start(out=out_part, in_=res[:, :, first:end, :])
 
-        prepare_w(0)
-        ready = front(0)
-        prepare_w(1)
-        prepare_w(2)
-        for n in range(N_CHUNKS):
-            following = front(n + 1) if n + 1 < N_CHUNKS else None
-            back(n, ready)
-            ready = following
+        copies = spread(gain_row[:])
+        nc.vector.tensor_copy(out=gain[:], in_=copies[:])
+        square_sums(0)
+        root(0)
+        invert(0)
+        scale_and_gain(0)
+        square_sums(1)
+        root(1)
+        transpose_w(0)
+        transpose(0)
+        quantise_w(0, [nc.vector.tensor_copy, nc.scalar.copy])
+        empty(0)
+        invert(1)
+        scale_and_gain(1)
+        transpose(1)
+        empty(1)
+        quantise(0)
+        quantise(1)
+        spread_bias(0)
+        multiply_gain(2)
+        multiply_gain(3)
+        transpose_w(1)
+        quantise_w(1, [nc.vector.tensor_copy, nc.scalar.copy])
+        square_sums(2)
+        root(2)
+        invert(2)
+        scale(2)
+        spread_bias(1)
+        transpose_w(2)
+        quantise_w(2, [nc.vector.tensor_copy, nc.scalar.copy])
+        spread_bias(2)
+        square_sums(3)
+        root(3)
+        multiply(0)
+        transpose(2)
+        multiply(1)
+
+        stack.enter_context(tc.manual_schedule())
+        for s in range(N_PAIRS):
+            if s + 2 < N_PAIRS:
+                empty(s + 2)
+            add_bias(2 * s)
+            if s + 3 < N_PAIRS:
+                invert(s + 3)
+                scale(s + 3)
+            if s + 2 < N_PAIRS:
+                quantise(s + 2)
+            if s + 4 < N_PAIRS:
+                square_sums(s + 4)
+                root(s + 4)
+                multiply_gain(s + 4)
+            if 2 * s + 2 < N_GROUPS:
+                multiply(2 * s + 2)
+            add_bias(2 * s + 1)
+            if s + 3 < N_PAIRS:
+                transpose(s + 3)
+            if 2 * s + 3 < N_GROUPS:
+                multiply(2 * s + 3)

@@ -23,9 +23,10 @@ PAIR = 2
 N_CHUNKS = B * ROWS // CHUNK
 N_PAIRS = B * ROWS // PAIR
 CHUNK_BANKS = 3 * CHUNK
-SHARED = 5
-GROUP = 3
-N_GROUPS = N_CHUNKS * CHUNK_BANKS // GROUP
+GROUPS = [list(range(k, k + 2)) for k in range(0, CHUNK_BANKS, 2)] + [
+    list(range(k, k + 3)) for k in range(CHUNK_BANKS, N_CHUNKS * CHUNK_BANKS, 3)
+]
+SHARED_BANKS = [group[0] for group in GROUPS[6:] if group[0] % CHUNK_BANKS == 0 or group[0] >= 78]
 W_TILES = D // P
 
 FLOPS = 2 * S * B * D * 3 * D
@@ -39,39 +40,44 @@ def tile_transformerblock_pa_t_kernel(tc, x, w_norm1, in_proj_w, in_proj_b, out_
 
     with ExitStack() as stack:
         const = stack.enter_context(tc.tile_pool(name="const", bufs=1))
-        xin = stack.enter_context(tc.tile_pool(name="xin", bufs=N_CHUNKS))
+        xin = stack.enter_context(tc.tile_pool(name="xin", bufs=1))
         wprep = stack.enter_context(tc.tile_pool(name="wprep", bufs=3))
         stat = stack.enter_context(tc.tile_pool(name="stat", bufs=6))
         work = stack.enter_context(tc.tile_pool(name="work", bufs=6))
         result = stack.enter_context(tc.tile_pool(name="result", bufs=6))
         psum_t = stack.enter_context(tc.psum_pool(name="psum_t", bufs=2))
         psum_o = stack.enter_context(tc.psum_pool(name="psum_o", bufs=6))
+        stack.enter_context(tc.manual_schedule())
 
         gain_row = const.tile([P, D], BF16)
-        nc.vector.memset(gain_row[:], 0.0)
-        nc.sync.dma_start(out=gain_row[0:1, :], in_=w_norm1.unsqueeze(0))
+        nc.vector.memset(gain_row[:].bitcast(I32), 0)
         bias_row = const.tile([P, 3 * D], BF16)
         nc.gpsimd.memset(bias_row[:].bitcast(I32), 0)
 
-        def load_x(n):
-            b, jq = divmod(n, ROWS // CHUNK)
-            xc = xin.tile([P, CHUNK, D], BF16, name="xc")
-            nc.sync.dma_start(out=xc[:], in_=x_view[:, jq * CHUNK : (jq + 1) * CHUNK, b, :])
-            return xc
+        x_tiles, w_raws = {}, []
+
+        def load_x(t, tiles):
+            b, j = divmod(t, ROWS)
+            xc = xin.tile([P, tiles, D], BF16, name="x%d" % t)
+            nc.sync.dma_start(out=xc[:], in_=x_view[:, j : j + tiles, b, :])
+            for i in range(tiles):
+                x_tiles[t + i] = xc[:, i, :]
 
         def load_w(c):
             w_raw = wprep.tile([P, W_TILES, D], BF16, name="w_raw")
             nc.sync.dma_start(out=w_raw[:], in_=w_view[c])
-            return w_raw
+            w_raws.append(w_raw)
 
-        x_chunks = [load_x(0)]
-        w_raws = [load_w(0)]
-        x_chunks.append(load_x(1))
+        load_x(0, PAIR)
+        nc.sync.dma_start(out=gain_row[0:1, :], in_=w_norm1.unsqueeze(0))
+        load_w(0)
+        load_x(PAIR, PAIR)
+        load_w(1)
         nc.sync.dma_start(out=bias_row[0:1, :], in_=in_proj_b.unsqueeze(0))
-        w_raws.append(load_w(1))
-        w_raws.append(load_w(2))
+        load_x(CHUNK, CHUNK)
+        load_w(2)
         for n in range(2, N_CHUNKS):
-            x_chunks.append(load_x(n))
+            load_x(n * CHUNK, CHUNK)
 
         ident_f32 = const.tile([P, P], F32)
         make_identity(nc, ident_f32[:])
@@ -95,42 +101,54 @@ def tile_transformerblock_pa_t_kernel(tc, x, w_norm1, in_proj_w, in_proj_b, out_
             copies = spread(bias_row[:, cols])
             nc.scalar.copy(out=bias[:, cols], in_=copies[:])
 
-        w_codes, w_scales, w_banks = {}, {}, {}
+        w_banks, w_groups, w_codes, w_scales = {}, {}, {}, {}
 
-        def transpose_w(c):
-            w_banks[c] = []
-            for half in range(W_TILES // PAIR):
+        def transpose_w(c, halves):
+            for half in halves:
                 wt = psum_o.tile([P, PAIR, 2, P], F32, name="wt", tag="acc")
                 for i in range(PAIR):
                     row_words = w_raws[c][:, half * PAIR + i, :].bitcast(F32)
                     for u in range(2):
                         nc.tensor.transpose(wt[:, i, u, :], row_words[:, u : 2 * P : 2], ident_f32[:])
-                w_banks[c].append(wt)
+                w_banks[c, half] = wt
 
-        def quantise_w(c, copies):
-            w_grouped = wprep.tile([P, D * PACK], BF16, name="w_grouped", align_bytes=64)
-            words = w_grouped[:].bitcast(F32).rearrange("p (a r u) -> p a r u", a=W_TILES, u=2)
-            for half, copy in enumerate(copies):
+        def empty_w(c):
+            w_groups[c] = wprep.tile([P, D * PACK], BF16, name="w_grouped", align_bytes=64)
+            words = w_groups[c][:].bitcast(F32).rearrange("p (a r u) -> p a r u", a=W_TILES, u=2)
+            for half, copy in enumerate([nc.vector.tensor_copy, nc.scalar.copy]):
                 copy(
                     out=words[:, half * PAIR : (half + 1) * PAIR, :, :],
-                    in_=w_banks[c][half][:].rearrange("p a u r -> p a r u"),
+                    in_=w_banks[c, half][:].rearrange("p a u r -> p a r u"),
                 )
-            codes = const.tile([P, D], U32, name="w_codes%d" % c, align_bytes=64)
-            scales = const.tile([P, D], U8, name="w_scales%d" % c, align_bytes=64)
-            nc.vector.quantize_mx(out=codes[:].bitcast(FP8X4), scales=scales[:], in_=w_grouped[:])
-            w_codes[c] = codes
-            w_scales[c] = scales
+
+        def quantise_w(c):
+            w_codes[c] = const.tile([P, D], U32, name="w_codes%d" % c, align_bytes=64)
+            w_scales[c] = const.tile([P, D], U8, name="w_scales%d" % c, align_bytes=64)
+            nc.vector.quantize_mx(out=w_codes[c][:].bitcast(FP8X4), scales=w_scales[c][:], in_=w_groups[c][:])
 
         sums, roots, rstds, products, hs, banks, groupeds, operands = {}, {}, {}, {}, {}, {}, {}, {}
 
         def x_tile(q, i):
-            return x_chunks[q * PAIR // CHUNK][:, q * PAIR % CHUNK + i, :]
+            return x_tiles[q * PAIR + i]
 
-        def square_sums(q):
-            sums[q] = stat.tile([P, PAIR], F32, name="sumsq")
-            for i in range(PAIR):
+        def square_sums(q, tiles=range(PAIR)):
+            if q not in sums:
+                sums[q] = stat.tile([P, PAIR], F32, name="sumsq")
+            for i in tiles:
                 squares = stat.tile([P, D], BF16, name="squares")
                 nc.scalar.activation(out=squares[:], in_=x_tile(q, i), func=ACT.Square, accum_out=sums[q][:, i : i + 1])
+
+        def square_sum_on_vector(q, i):
+            squares = stat.tile([P, D], BF16, name="squares")
+            nc.vector.scalar_tensor_tensor(
+                out=squares[:],
+                in0=x_tile(q, i),
+                scalar=1.0,
+                in1=x_tile(q, i),
+                op0=ALU.mult,
+                op1=ALU.mult,
+                accum_out=sums[q][:, i : i + 1],
+            )
 
         def root(q):
             roots[q] = stat.tile([P, PAIR], F32, name="rms")
@@ -193,7 +211,7 @@ def tile_transformerblock_pa_t_kernel(tc, x, w_norm1, in_proj_w, in_proj_b, out_
             return n, c, j
 
         def multiply(g):
-            for k in range(g * GROUP, (g + 1) * GROUP):
+            for k in GROUPS[g]:
                 n, c, j = place(k)
                 codes, scales = operands[(n * CHUNK + j) // PAIR]
                 cols = slice((j % PAIR) * P, (j % PAIR + 1) * P)
@@ -210,14 +228,16 @@ def tile_transformerblock_pa_t_kernel(tc, x, w_norm1, in_proj_w, in_proj_b, out_
                 accs[k] = acc
 
         def add_bias(g):
-            for k in [g * GROUP + i for i in (2, 0, 1)]:
+            shared = [k for k in GROUPS[g] if k in SHARED_BANKS]
+            own = [k for k in GROUPS[g] if k not in SHARED_BANKS]
+            for k in shared + own[-1:] + own[:-1]:
                 n, c, j = place(k)
                 if (n, c) not in results:
                     results[n, c] = (result.tile([P, HEADS, CHUNK, HD], F32, name="res"), [])
                 res, done = results[n, c]
                 sums_in = accs[k][:].rearrange("p (h d) -> p h d", h=HEADS)
                 bias_in = bias[:, c * D : (c + 1) * D].rearrange("p (h d) -> p h d", h=HEADS)
-                if k % CHUNK_BANKS == SHARED:
+                if k in SHARED_BANKS:
                     nc.scalar.copy(out=res[:, :, j, :], in_=sums_in)
                     nc.gpsimd.tensor_tensor(out=res[:, :, j, :], in0=res[:, :, j, :], in1=bias_in, op=ALU.add)
                 else:
@@ -232,48 +252,83 @@ def tile_transformerblock_pa_t_kernel(tc, x, w_norm1, in_proj_w, in_proj_b, out_
                         out_part = out_view[:, :, jq * CHUNK + first : jq * CHUNK + end, :]
                         nc.sync.dma_start(out=out_part, in_=res[:, :, first:end, :])
 
+        square_sums(0, (0,))
+        square_sum_on_vector(0, 1)
+        root(0)
         copies = spread(gain_row[:])
         nc.vector.tensor_copy(out=gain[:], in_=copies[:])
-        square_sums(0)
-        root(0)
         invert(0)
         scale_and_gain(0)
         square_sums(1)
         root(1)
-        transpose_w(0)
+        transpose_w(0, (0, 1))
+        empty_w(0)
         transpose(0)
-        quantise_w(0, [nc.vector.tensor_copy, nc.scalar.copy])
         empty(0)
+        spread_bias(0)
+        quantise_w(0)
+        quantise(0)
+        multiply(0)
+        square_sums(2)
+        root(2)
         invert(1)
         scale_and_gain(1)
         transpose(1)
-        empty(1)
-        quantise(0)
-        quantise(1)
-        spread_bias(0)
+        square_sums(3, (0,))
+        transpose_w(1, (0, 1))
         multiply_gain(2)
         multiply_gain(3)
-        transpose_w(1)
-        quantise_w(1, [nc.vector.tensor_copy, nc.scalar.copy])
-        square_sums(2)
-        root(2)
         invert(2)
-        scale(2)
-        spread_bias(1)
-        transpose_w(2)
-        quantise_w(2, [nc.vector.tensor_copy, nc.scalar.copy])
-        spread_bias(2)
-        square_sums(3)
-        root(3)
-        multiply(0)
-        transpose(2)
+        empty(1)
+        add_bias(0)
+        quantise(1)
+        empty_w(1)
+        quantise_w(1)
         multiply(1)
+        spread_bias(1)
+        scale(2)
+        transpose_w(2, (0,))
+        multiply(2)
+        square_sums(3, (1,))
+        root(3)
+        transpose_w(2, (1,))
+        add_bias(1)
+        transpose(2)
+        empty_w(2)
+        multiply(3)
+        invert(3)
+        spread_bias(2)
+        empty(2)
+        add_bias(2)
+        quantise_w(2)
+        quantise(2)
+        scale(3)
+        add_bias(3)
+        multiply(4)
+        transpose(3)
+        multiply(5)
+        square_sums(4, (0,))
+        empty(3)
+        square_sums(4, (1,))
+        root(4)
+        multiply_gain(4)
+        add_bias(4)
+        quantise(3)
+        invert(4)
+        scale(4)
+        square_sums(5)
+        root(5)
+        multiply_gain(5)
+        multiply(6)
+        add_bias(5)
+        transpose(4)
+        multiply(7)
 
-        stack.enter_context(tc.manual_schedule())
-        for s in range(N_PAIRS):
+        for s in range(2, N_PAIRS):
+            g = 2 * s + 2
             if s + 2 < N_PAIRS:
                 empty(s + 2)
-            add_bias(2 * s)
+            add_bias(g)
             if s + 3 < N_PAIRS:
                 invert(s + 3)
                 scale(s + 3)
@@ -283,10 +338,10 @@ def tile_transformerblock_pa_t_kernel(tc, x, w_norm1, in_proj_w, in_proj_b, out_
                 square_sums(s + 4)
                 root(s + 4)
                 multiply_gain(s + 4)
-            if 2 * s + 2 < N_GROUPS:
-                multiply(2 * s + 2)
-            add_bias(2 * s + 1)
+            if g + 2 < len(GROUPS):
+                multiply(g + 2)
+            add_bias(g + 1)
             if s + 3 < N_PAIRS:
                 transpose(s + 3)
-            if 2 * s + 3 < N_GROUPS:
-                multiply(2 * s + 3)
+            if g + 3 < len(GROUPS):
+                multiply(g + 3)

@@ -84,7 +84,7 @@ def tile_transformerblock_pa_t_kernel(tc, x, w_norm1, in_proj_w, in_proj_b, out_
         eps = const.tile([P, 1], F32)
         nc.vector.memset(eps[:], EPS)
         warm = const.tile([P, 1], F32)
-        nc.scalar.activation(out=warm[:], in_=eps[:], func=ACT.Sqrt)
+        nc.scalar.activation(out=warm[:], in_=eps[:], func=ACT.Abs_reciprocal_sqrt)
 
         ones = const.tile([P, P], BF16)
         nc.vector.memset(ones[:], 1.0)
@@ -96,10 +96,10 @@ def tile_transformerblock_pa_t_kernel(tc, x, w_norm1, in_proj_w, in_proj_b, out_
             nc.tensor.matmul(out=copies[:], lhsT=ones[:], rhs=row, start=True, stop=True)
             return copies
 
-        def spread_bias(c):
+        def spread_bias(c, copy):
             cols = slice(c * D, (c + 1) * D)
             copies = spread(bias_row[:, cols])
-            nc.scalar.copy(out=bias[:, cols], in_=copies[:])
+            copy(out=bias[:, cols], in_=copies[:])
 
         w_banks, w_groups, w_codes, w_scales = {}, {}, {}, {}
 
@@ -112,10 +112,10 @@ def tile_transformerblock_pa_t_kernel(tc, x, w_norm1, in_proj_w, in_proj_b, out_
                         nc.tensor.transpose(wt[:, i, u, :], row_words[:, u : 2 * P : 2], ident_f32[:])
                 w_banks[c, half] = wt
 
-        def empty_w(c):
+        def empty_w(c, copies):
             w_groups[c] = wprep.tile([P, D * PACK], BF16, name="w_grouped", align_bytes=64)
             words = w_groups[c][:].bitcast(F32).rearrange("p (a r u) -> p a r u", a=W_TILES, u=2)
-            for half, copy in enumerate([nc.vector.tensor_copy, nc.scalar.copy]):
+            for half, copy in enumerate(copies):
                 copy(
                     out=words[:, half * PAIR : (half + 1) * PAIR, :, :],
                     in_=w_banks[c, half][:].rearrange("p a u r -> p a r u"),
@@ -126,7 +126,7 @@ def tile_transformerblock_pa_t_kernel(tc, x, w_norm1, in_proj_w, in_proj_b, out_
             w_scales[c] = const.tile([P, D], U8, name="w_scales%d" % c, align_bytes=64)
             nc.vector.quantize_mx(out=w_codes[c][:].bitcast(FP8X4), scales=w_scales[c][:], in_=w_groups[c][:])
 
-        sums, roots, rstds, products, hs, banks, groupeds, operands = {}, {}, {}, {}, {}, {}, {}, {}
+        sums, rstds, products, hs, banks, groupeds, operands = {}, {}, {}, {}, {}, {}, {}
 
         def x_tile(q, i):
             return x_tiles[q * PAIR + i]
@@ -151,12 +151,10 @@ def tile_transformerblock_pa_t_kernel(tc, x, w_norm1, in_proj_w, in_proj_b, out_
             )
 
         def root(q):
-            roots[q] = stat.tile([P, PAIR], F32, name="rms")
-            nc.scalar.activation(out=roots[q][:], in_=sums[q][:], func=ACT.Sqrt, scale=1.0 / D, bias=eps[:])
-
-        def invert(q):
             rstds[q] = stat.tile([P, PAIR], F32, name="rstd")
-            nc.vector.reciprocal(out=rstds[q][:], in_=roots[q][:])
+            nc.scalar.activation(
+                out=rstds[q][:], in_=sums[q][:], func=ACT.Abs_reciprocal_sqrt, scale=1.0 / D, bias=eps[:]
+            )
 
         def multiply_gain(q):
             products[q] = []
@@ -257,71 +255,66 @@ def tile_transformerblock_pa_t_kernel(tc, x, w_norm1, in_proj_w, in_proj_b, out_
         root(0)
         copies = spread(gain_row[:])
         nc.vector.tensor_copy(out=gain[:], in_=copies[:])
-        invert(0)
         scale_and_gain(0)
         square_sums(1)
         root(1)
         transpose_w(0, (0, 1))
-        empty_w(0)
+        empty_w(0, (nc.vector.tensor_copy, nc.scalar.copy))
         transpose(0)
         empty(0)
-        spread_bias(0)
+        spread_bias(0, nc.scalar.copy)
         quantise_w(0)
         quantise(0)
         multiply(0)
         square_sums(2)
         root(2)
-        invert(1)
         scale_and_gain(1)
         transpose(1)
         square_sums(3, (0,))
         transpose_w(1, (0, 1))
         multiply_gain(2)
         multiply_gain(3)
-        invert(2)
         empty(1)
         add_bias(0)
         quantise(1)
-        empty_w(1)
+        empty_w(1, (nc.vector.tensor_copy, nc.scalar.copy))
         quantise_w(1)
         multiply(1)
-        spread_bias(1)
+        spread_bias(1, nc.vector.tensor_copy)
         scale(2)
         transpose_w(2, (0,))
         multiply(2)
         square_sums(3, (1,))
         root(3)
+        transpose(2)
         transpose_w(2, (1,))
         add_bias(1)
-        transpose(2)
-        empty_w(2)
+        empty_w(2, (nc.vector.tensor_copy, nc.vector.tensor_copy))
         multiply(3)
-        invert(3)
-        spread_bias(2)
+        spread_bias(2, nc.vector.tensor_copy)
         empty(2)
+        scale(3)
+        transpose(3)
         add_bias(2)
         quantise_w(2)
         quantise(2)
-        scale(3)
-        add_bias(3)
-        multiply(4)
-        transpose(3)
-        multiply(5)
         square_sums(4, (0,))
         empty(3)
+        add_bias(3)
+        multiply(4)
+        multiply(5)
         square_sums(4, (1,))
         root(4)
         multiply_gain(4)
-        add_bias(4)
-        quantise(3)
-        invert(4)
         scale(4)
+        transpose(4)
+        quantise(3)
+        add_bias(4)
         square_sums(5)
         root(5)
         multiply_gain(5)
         multiply(6)
         add_bias(5)
-        transpose(4)
         multiply(7)
 
         for s in range(2, N_PAIRS):
@@ -330,7 +323,6 @@ def tile_transformerblock_pa_t_kernel(tc, x, w_norm1, in_proj_w, in_proj_b, out_
                 empty(s + 2)
             add_bias(g)
             if s + 3 < N_PAIRS:
-                invert(s + 3)
                 scale(s + 3)
             if s + 2 < N_PAIRS:
                 quantise(s + 2)

@@ -43,7 +43,7 @@ def tile_transformerblock_pa_t_kernel(tc, x, w_norm1, in_proj_w, in_proj_b, out_
         xin = stack.enter_context(tc.tile_pool(name="xin", bufs=1))
         wprep = stack.enter_context(tc.tile_pool(name="wprep", bufs=3))
         stat = stack.enter_context(tc.tile_pool(name="stat", bufs=6))
-        work = stack.enter_context(tc.tile_pool(name="work", bufs=6))
+        work = stack.enter_context(tc.tile_pool(name="work", bufs=8))
         result = stack.enter_context(tc.tile_pool(name="result", bufs=6))
         psum_t = stack.enter_context(tc.psum_pool(name="psum_t", bufs=2))
         psum_o = stack.enter_context(tc.psum_pool(name="psum_o", bufs=6))
@@ -91,15 +91,13 @@ def tile_transformerblock_pa_t_kernel(tc, x, w_norm1, in_proj_w, in_proj_b, out_
         gain = const.tile([P, D], BF16)
         bias = const.tile([P, 3 * D], BF16)
 
-        def spread(row):
-            copies = psum_o.tile([P, D], F32, name="copies", tag="acc")
-            nc.tensor.matmul(out=copies[:], lhsT=ones[:], rhs=row, start=True, stop=True)
-            return copies
-
-        def spread_bias(c, copy):
-            cols = slice(c * D, (c + 1) * D)
-            copies = spread(bias_row[:, cols])
-            copy(out=bias[:, cols], in_=copies[:])
+        def spread(row, everywhere):
+            copies = psum_o.tile([P, 2 * D], BF16, name="copies", tag="acc")
+            width = row.shape[1]
+            for first in range(0, width, D):
+                part = slice(first, first + D)
+                nc.tensor.matmul(out=copies[:, part], lhsT=ones[:], rhs=row[:, part], start=True, stop=True)
+            nc.vector.tensor_copy(out=everywhere, in_=copies[:, :width])
 
         w_banks, w_groups, w_codes, w_scales = {}, {}, {}, {}
 
@@ -253,8 +251,7 @@ def tile_transformerblock_pa_t_kernel(tc, x, w_norm1, in_proj_w, in_proj_b, out_
         square_sums(0, (0,))
         square_sum_on_vector(0, 1)
         root(0)
-        copies = spread(gain_row[:])
-        nc.vector.tensor_copy(out=gain[:], in_=copies[:])
+        spread(gain_row[:], gain[:])
         scale_and_gain(0)
         square_sums(1)
         root(1)
@@ -262,58 +259,57 @@ def tile_transformerblock_pa_t_kernel(tc, x, w_norm1, in_proj_w, in_proj_b, out_
         empty_w(0, (nc.vector.tensor_copy, nc.scalar.copy))
         transpose(0)
         empty(0)
-        spread_bias(0, nc.scalar.copy)
         quantise_w(0)
         quantise(0)
+        spread(bias_row[:, :D], bias[:, :D])
         multiply(0)
         square_sums(2)
         root(2)
         scale_and_gain(1)
         transpose(1)
-        square_sums(3, (0,))
+        square_sums(3)
         transpose_w(1, (0, 1))
         multiply_gain(2)
         multiply_gain(3)
+        multiply_gain(4)
+        multiply_gain(5)
         empty(1)
+        root(3)
         add_bias(0)
         quantise(1)
         empty_w(1, (nc.vector.tensor_copy, nc.scalar.copy))
         quantise_w(1)
         multiply(1)
-        spread_bias(1, nc.vector.tensor_copy)
+        spread(bias_row[:, D:], bias[:, D:])
         scale(2)
         transpose_w(2, (0,))
         multiply(2)
-        square_sums(3, (1,))
-        root(3)
         transpose(2)
         transpose_w(2, (1,))
-        add_bias(1)
-        empty_w(2, (nc.vector.tensor_copy, nc.vector.tensor_copy))
         multiply(3)
-        spread_bias(2, nc.vector.tensor_copy)
+        add_bias(1)
+        add_bias(2)
+        empty_w(2, (nc.scalar.copy, nc.vector.tensor_copy))
         empty(2)
         scale(3)
         transpose(3)
-        add_bias(2)
         quantise_w(2)
         quantise(2)
         square_sums(4, (0,))
         empty(3)
-        add_bias(3)
         multiply(4)
+        add_bias(3)
         multiply(5)
         square_sums(4, (1,))
         root(4)
-        multiply_gain(4)
         scale(4)
-        transpose(4)
-        quantise(3)
         add_bias(4)
+        quantise(3)
         square_sums(5)
         root(5)
-        multiply_gain(5)
+        multiply_gain(6)
         multiply(6)
+        transpose(4)
         add_bias(5)
         multiply(7)
 
@@ -329,7 +325,8 @@ def tile_transformerblock_pa_t_kernel(tc, x, w_norm1, in_proj_w, in_proj_b, out_
             if s + 4 < N_PAIRS:
                 square_sums(s + 4)
                 root(s + 4)
-                multiply_gain(s + 4)
+            if s + 5 < N_PAIRS:
+                multiply_gain(s + 5)
             if g + 2 < len(GROUPS):
                 multiply(g + 2)
             add_bias(g + 1)

@@ -165,7 +165,12 @@ def tile_transformerblock_pa_t_kernel(tc, x, w_norm1, in_proj_w, in_proj_b, out_
             hs[q] = []
             for i in range(PAIR):
                 h = work.tile([P, D], BF16, name="h")
-                nc.scalar.activation(out=h[:], in_=products[q][i][:], func=ACT.Copy, scale=rstds[q][:, i : i + 1])
+                nc.scalar.activation(
+                    out=h[:].rearrange("p (u w e) -> p u w e", u=2, e=2),
+                    in_=products[q][i][:].rearrange("p (w u e) -> p u w e", u=2, e=2),
+                    func=ACT.Copy,
+                    scale=rstds[q][:, i : i + 1],
+                )
                 hs[q].append(h)
 
         def scale_and_gain(q):
@@ -182,7 +187,8 @@ def tile_transformerblock_pa_t_kernel(tc, x, w_norm1, in_proj_w, in_proj_b, out_
             for i in range(PAIR):
                 h_words = hs[q][i][:].bitcast(F32)
                 for u in range(2):
-                    nc.tensor.transpose(ht[:, i, u, :], h_words[:, u : 2 * P : 2], ident_f32[:])
+                    words = h_words[:, u : 2 * P : 2] if q < 2 else h_words[:, u * P : (u + 1) * P]
+                    nc.tensor.transpose(ht[:, i, u, :], words, ident_f32[:])
             banks[q] = ht
 
         def empty(q):

from contextlib import ExitStack

import concourse.mybir as mybir
from concourse.masks import make_identity

F32 = mybir.dt.float32
BF16 = mybir.dt.bfloat16
U32 = mybir.dt.uint32
U8 = mybir.dt.uint8
I32 = mybir.dt.int32
FP8X4 = mybir.dt.float8_e4m3fn_x4
ACT = mybir.ActivationFunctionType
ALU = mybir.AluOpType

P = 128
S, B, D = 1024, 4, 512
HEADS, HD = 2, 256
EPS = 1e-8
PACK = 4
ROWS = S // P
CHUNK = 4
PAIR = 2
N_CHUNKS = B * ROWS // CHUNK
N_PAIRS = B * ROWS // PAIR
CHUNK_BANKS = 3 * CHUNK
GROUPS = [list(range(k, k + 2)) for k in range(0, CHUNK_BANKS, 2)] + [
    list(range(k, k + 3)) for k in range(CHUNK_BANKS, N_CHUNKS * CHUNK_BANKS, 3)
]
SHARED_BANKS = [group[0] for group in GROUPS[6:] if group[0] % CHUNK_BANKS == 0 or group[0] >= 78]
W_TILES = D // P

FLOPS = 2 * S * B * D * 3 * D


def tile_transformerblock_pa_t_kernel(tc, x, w_norm1, in_proj_w, in_proj_b, out_0, out_1, out_2):
    nc = tc.nc
    outs = [out_0, out_1, out_2]
    x_view = x.rearrange("(p j) b d -> p j b d", j=ROWS)
    w_view = in_proj_w.rearrange("(c a p) d -> c p a d", c=3, a=W_TILES)

    with ExitStack() as stack:
        const = stack.enter_context(tc.tile_pool(name="const", bufs=1))
        xin = stack.enter_context(tc.tile_pool(name="xin", bufs=1))
        wprep = stack.enter_context(tc.tile_pool(name="wprep", bufs=3))
        stat = stack.enter_context(tc.tile_pool(name="stat", bufs=6))
        work = stack.enter_context(tc.tile_pool(name="work", bufs=8))
        result = stack.enter_context(tc.tile_pool(name="result", bufs=6))
        psum_t = stack.enter_context(tc.psum_pool(name="psum_t", bufs=2))
        psum_o = stack.enter_context(tc.psum_pool(name="psum_o", bufs=6))
        stack.enter_context(tc.manual_schedule())

        gain_row = const.tile([P, D], BF16)
        nc.vector.memset(gain_row[:].bitcast(I32), 0)
        bias_row = const.tile([P, 3 * D], BF16)
        nc.gpsimd.memset(bias_row[:].bitcast(I32), 0)

        x_tiles, w_raws = {}, []

        def load_x(t, tiles):
            b, j = divmod(t, ROWS)
            xc = xin.tile([P, tiles, D], BF16, name="x%d" % t)
            nc.sync.dma_start(out=xc[:], in_=x_view[:, j : j + tiles, b, :])
            for i in range(tiles):
                x_tiles[t + i] = xc[:, i, :]

        def load_w(c):
            w_raw = wprep.tile([P, W_TILES, D], BF16, name="w_raw")
            nc.sync.dma_start(out=w_raw[:], in_=w_view[c])
            w_raws.append(w_raw)

        load_x(0, PAIR)
        nc.sync.dma_start(out=gain_row[0:1, :], in_=w_norm1.unsqueeze(0))
        load_w(0)
        load_x(PAIR, PAIR)
        load_w(1)
        nc.sync.dma_start(out=bias_row[0:1, :], in_=in_proj_b.unsqueeze(0))
        load_x(CHUNK, CHUNK)
        load_w(2)
        for n in range(2, N_CHUNKS):
            load_x(n * CHUNK, CHUNK)

        ident_f32 = const.tile([P, P], F32)
        make_identity(nc, ident_f32[:])
        eps = const.tile([P, 1], F32)
        nc.vector.memset(eps[:], EPS)
        warm = const.tile([P, 1], F32)
        nc.scalar.activation(out=warm[:], in_=eps[:], func=ACT.Abs_reciprocal_sqrt)

        ones = const.tile([P, P], BF16)
        nc.vector.memset(ones[:], 1.0)
        gain = const.tile([P, D], BF16)
        bias = const.tile([P, 3 * D], BF16)

        def spread(row, everywhere):
            copies = psum_o.tile([P, 2 * D], BF16, name="copies", tag="acc")
            width = row.shape[1]
            for first in range(0, width, D):
                part = slice(first, first + D)
                nc.tensor.matmul(out=copies[:, part], lhsT=ones[:], rhs=row[:, part], start=True, stop=True)
            nc.vector.tensor_copy(out=everywhere, in_=copies[:, :width])

        w_banks, w_groups, w_codes, w_scales = {}, {}, {}, {}

        def transpose_w(c, halves):
            for half in halves:
                wt = psum_o.tile([P, PAIR, 2, P], F32, name="wt", tag="acc")
                for i in range(PAIR):
                    row_words = w_raws[c][:, half * PAIR + i, :].bitcast(F32)
                    for u in range(2):
                        nc.tensor.transpose(wt[:, i, u, :], row_words[:, u : 2 * P : 2], ident_f32[:])
                w_banks[c, half] = wt

        def empty_w(c, copies):
            w_groups[c] = wprep.tile([P, D * PACK], BF16, name="w_grouped", align_bytes=64)
            words = w_groups[c][:].bitcast(F32).rearrange("p (a r u) -> p a r u", a=W_TILES, u=2)
            for half, copy in enumerate(copies):
                copy(
                    out=words[:, half * PAIR : (half + 1) * PAIR, :, :],
                    in_=w_banks[c, half][:].rearrange("p a u r -> p a r u"),
                )

        def quantise_w(c):
            w_codes[c] = const.tile([P, D], U32, name="w_codes%d" % c, align_bytes=64)
            w_scales[c] = const.tile([P, D], U8, name="w_scales%d" % c, align_bytes=64)
            nc.vector.quantize_mx(out=w_codes[c][:].bitcast(FP8X4), scales=w_scales[c][:], in_=w_groups[c][:])

        sums, rstds, products, hs, banks, groupeds, operands = {}, {}, {}, {}, {}, {}, {}

        def x_tile(q, i):
            return x_tiles[q * PAIR + i]

        def square_sums(q, tiles=range(PAIR)):
            if q not in sums:
                sums[q] = stat.tile([P, PAIR], F32, name="sumsq")
            for i in tiles:
                squares = stat.tile([P, D], BF16, name="squares")
                nc.scalar.activation(out=squares[:], in_=x_tile(q, i), func=ACT.Square, accum_out=sums[q][:, i : i + 1])

        def square_sum_on_vector(q, i):
            squares = stat.tile([P, D], BF16, name="squares")
            nc.vector.scalar_tensor_tensor(
                out=squares[:],
                in0=x_tile(q, i),
                scalar=1.0,
                in1=x_tile(q, i),
                op0=ALU.mult,
                op1=ALU.mult,
                accum_out=sums[q][:, i : i + 1],
            )

        def root(q):
            rstds[q] = stat.tile([P, PAIR], F32, name="rstd")
            nc.scalar.activation(
                out=rstds[q][:], in_=sums[q][:], func=ACT.Abs_reciprocal_sqrt, scale=1.0 / D, bias=eps[:]
            )

        def multiply_gain(q):
            products[q] = []
            for i in range(PAIR):
                y = work.tile([P, D], F32, name="y")
                nc.gpsimd.tensor_tensor(out=y[:], in0=x_tile(q, i), in1=gain[:], op=ALU.mult)
                products[q].append(y)

        def scale(q):
            hs[q] = []
            for i in range(PAIR):
                h = work.tile([P, D], BF16, name="h")
                nc.scalar.activation(
                    out=h[:].rearrange("p (u w e) -> p u w e", u=2, e=2),
                    in_=products[q][i][:].rearrange("p (w u e) -> p u w e", u=2, e=2),
                    func=ACT.Copy,
                    scale=rstds[q][:, i : i + 1],
                )
                hs[q].append(h)

        def scale_and_gain(q):
            hs[q] = []
            for i in range(PAIR):
                h = work.tile([P, D], BF16, name="h")
                nc.vector.scalar_tensor_tensor(
                    out=h[:], in0=x_tile(q, i), scalar=rstds[q][:, i : i + 1], in1=gain[:], op0=ALU.mult, op1=ALU.mult
                )
                hs[q].append(h)

        def transpose(q):
            ht = psum_t.tile([P, PAIR, 2, P], F32, name="ht")
            for i in range(PAIR):
                h_words = hs[q][i][:].bitcast(F32)
                for u in range(2):
                    words = h_words[:, u : 2 * P : 2] if q < 2 else h_words[:, u * P : (u + 1) * P]
                    nc.tensor.transpose(ht[:, i, u, :], words, ident_f32[:])
            banks[q] = ht

        def empty(q):
            grouped = work.tile([P, PAIR * P * PACK], BF16, name="grouped", align_bytes=64)
            nc.scalar.copy(
                out=grouped[:].bitcast(F32).rearrange("p (i r u) -> p i r u", i=PAIR, u=2),
                in_=banks[q][:].rearrange("p i u r -> p i r u"),
            )
            groupeds[q] = grouped

        def quantise(q):
            codes = work.tile([P, PAIR * P], U32, name="h_codes", align_bytes=64)
            scales = work.tile([P, PAIR * P], U8, name="h_scales", align_bytes=64)
            nc.vector.quantize_mx(out=codes[:].bitcast(FP8X4), scales=scales[:], in_=groupeds[q][:])
            operands[q] = (codes, scales)

        accs, results = {}, {}

        def place(k):
            n, r = divmod(k, CHUNK_BANKS)
            c, j = divmod(r, CHUNK)
            return n, c, j

        def multiply(g):
            for k in GROUPS[g]:
                n, c, j = place(k)
                codes, scales = operands[(n * CHUNK + j) // PAIR]
                cols = slice((j % PAIR) * P, (j % PAIR + 1) * P)
                acc = psum_o.tile([P, D], F32, name="acc", tag="acc")
                nc.tensor.matmul_mx(
                    out=acc[:],
                    lhsT=codes[:, cols].bitcast(FP8X4),
                    lhsT_scale=scales[:, cols],
                    rhs=w_codes[c][:].bitcast(FP8X4),
                    rhs_scale=w_scales[c][:],
                    start=True,
                    stop=True,
                )
                accs[k] = acc

        def add_bias(g):
            shared = [k for k in GROUPS[g] if k in SHARED_BANKS]
            own = [k for k in GROUPS[g] if k not in SHARED_BANKS]
            for k in shared + own[-1:] + own[:-1]:
                n, c, j = place(k)
                if (n, c) not in results:
                    results[n, c] = (result.tile([P, HEADS, CHUNK, HD], F32, name="res"), [])
                res, done = results[n, c]
                sums_in = accs[k][:].rearrange("p (h d) -> p h d", h=HEADS)
                bias_in = bias[:, c * D : (c + 1) * D].rearrange("p (h d) -> p h d", h=HEADS)
                if k in SHARED_BANKS:
                    nc.scalar.copy(out=res[:, :, j, :], in_=sums_in)
                    nc.gpsimd.tensor_tensor(out=res[:, :, j, :], in0=res[:, :, j, :], in1=bias_in, op=ALU.add)
                else:
                    nc.vector.tensor_tensor(out=res[:, :, j, :], in0=sums_in, in1=bias_in, op=ALU.add)
                done.append(j)
                last = n == N_CHUNKS - 1 and c == 2
                for part in [(0, 1), (2, 3)] if last else [(0, 1, 2, 3)]:
                    if j in part and all(i in done for i in part):
                        b, jq = divmod(n, ROWS // CHUNK)
                        first, end = part[0], part[-1] + 1
                        out_view = outs[c][b].rearrange("h (p j) d -> p h j d", j=ROWS)
                        out_part = out_view[:, :, jq * CHUNK + first : jq * CHUNK + end, :]
                        nc.sync.dma_start(out=out_part, in_=res[:, :, first:end, :])

        square_sums(0, (0,))
        square_sum_on_vector(0, 1)
        root(0)
        spread(gain_row[:], gain[:])
        scale_and_gain(0)
        square_sums(1)
        root(1)
        transpose_w(0, (0, 1))
        empty_w(0, (nc.vector.tensor_copy, nc.scalar.copy))
        transpose(0)
        empty(0)
        quantise_w(0)
        quantise(0)
        spread(bias_row[:, :D], bias[:, :D])
        multiply(0)
        square_sums(2)
        root(2)
        scale_and_gain(1)
        transpose(1)
        square_sums(3)
        transpose_w(1, (0, 1))
        multiply_gain(2)
        multiply_gain(3)
        multiply_gain(4)
        multiply_gain(5)
        empty(1)
        root(3)
        add_bias(0)
        quantise(1)
        empty_w(1, (nc.vector.tensor_copy, nc.scalar.copy))
        quantise_w(1)
        multiply(1)
        spread(bias_row[:, D:], bias[:, D:])
        scale(2)
        transpose_w(2, (0,))
        multiply(2)
        transpose(2)
        transpose_w(2, (1,))
        multiply(3)
        add_bias(1)
        add_bias(2)
        empty_w(2, (nc.scalar.copy, nc.vector.tensor_copy))
        empty(2)
        scale(3)
        transpose(3)
        quantise_w(2)
        quantise(2)
        square_sums(4, (0,))
        empty(3)
        multiply(4)
        add_bias(3)
        multiply(5)
        square_sums(4, (1,))
        root(4)
        scale(4)
        add_bias(4)
        quantise(3)
        square_sums(5)
        root(5)
        multiply_gain(6)
        multiply(6)
        transpose(4)
        add_bias(5)
        multiply(7)

        for s in range(2, N_PAIRS):
            g = 2 * s + 2
            if s + 2 < N_PAIRS:
                empty(s + 2)
            add_bias(g)
            if s + 3 < N_PAIRS:
                scale(s + 3)
            if s + 2 < N_PAIRS:
                quantise(s + 2)
            if s + 4 < N_PAIRS:
                square_sums(s + 4)
                root(s + 4)
            if s + 5 < N_PAIRS:
                multiply_gain(s + 5)
            if g + 2 < len(GROUPS):
                multiply(g + 2)
            add_bias(g + 1)
            if s + 3 < N_PAIRS:
                transpose(s + 3)
            if g + 3 < len(GROUPS):
                multiply(g + 3)
